import numpy as np
import ml_dtypes


def mxq(x, axis, fmt="e4m3"):
    dtype, down = {"e4m3": (ml_dtypes.float8_e4m3fn, 7), "e5m2": (ml_dtypes.float8_e5m2, 14)}[fmt]
    v = np.moveaxis(np.asarray(x, np.float32).astype(ml_dtypes.bfloat16).astype(np.float64), axis, -1)
    blocks = v.reshape(v.shape[:-1] + (-1, 32))
    amax = np.abs(blocks).max(-1, keepdims=True)
    byte = np.maximum(np.where(amax > 0, np.frexp(amax)[1] - 1 + 127, 0) - down, 1)
    scale = np.exp2(byte - 127.0)
    codes = (blocks / scale).astype(np.float32).astype(dtype).astype(np.float64)
    return np.moveaxis((codes * scale).reshape(v.shape), -1, axis)


WIDE = False


def mx_kscale(k):
    if not WIDE:
        return np.ones(k)
    levels = np.array([10, -10, 5, -5, 0])
    if k % 512:
        return np.exp2(np.random.permutation(np.resize(levels, k // 32))).repeat(32)
    a = np.empty((k // 512, 16))
    for p in range(k // 512):
        a[p, :8] = np.random.permutation(np.resize(levels, 8))
        for g in range(8):
            far = levels[np.abs(levels - a[p, g]) >= 10]
            a[p, g + 8] = far[np.random.randint(len(far))]
    return np.exp2(a.ravel()).repeat(32)


BF16 = ml_dtypes.bfloat16


def bf(x):
    return np.asarray(x, np.float32).astype(BF16)


def f64(x):
    return np.asarray(x).astype(np.float64)


D, KW, STRIDE, STACK, B, O = 32, 11, 3, 8, 4096, 128
W_IN = D * D
POS = (D - KW) // STRIDE + 1
K = STACK * POS * POS


def build_mask():
    base_new = np.tile(np.arange(KW), KW)
    addition_new = np.repeat(np.arange(KW) * D, KW)
    index_1 = addition_new + base_new
    index_width = np.tile(index_1, POS)
    addition_width = np.repeat(STRIDE * np.arange(POS), KW * KW)
    index_row = index_width + addition_width
    index_column = np.tile(index_row, POS)
    addition_height = np.repeat(STRIDE * D * np.arange(POS), KW * KW * POS)
    index_final = index_column + addition_height
    stack = np.repeat(np.arange(POS * POS), KW * KW)
    block = np.zeros((POS * POS, W_IN))
    block[stack, index_final] = 1.0
    return np.vstack([block] * STACK)


def setup_inputs():
    s = mx_kscale(W_IN)
    return {"z": bf(np.random.standard_normal((B, W_IN)) * s),
            "T1": bf(np.random.standard_normal((K, W_IN)) * 0.7 / np.sqrt(KW * KW) / s),
            "T2": bf(np.random.standard_normal((K, W_IN)) * 0.7 / np.sqrt(KW * KW) / s),
            "T0": bf(np.random.standard_normal(K)),
            "mask": bf(build_mask())}


def reference(z, T1, T2, T0, mask):
    zq = mxq(f64(z).reshape(-1, D * D), 1, "e4m3")
    m = f64(mask)
    x1 = zq @ mxq(m * f64(T1), 1, "e4m3").T
    x2 = 2.0 * (zq @ mxq(m * f64(T2), 1, "e4m3").T) * x1 - f64(T0)
    return x1, x2

@@ -1,0 +1,267 @@
+from contextlib import ExitStack
+
+import concourse.mybir as mybir
+from concourse.masks import make_identity
+
+F32 = mybir.dt.float32
+BF16 = mybir.dt.bfloat16
+U32 = mybir.dt.uint32
+U8 = mybir.dt.uint8
+FP8X4 = mybir.dt.float8_e4m3fn_x4
+ALU = mybir.AluOpType
+
+P = 128
+B, K, O = 4096, 1024, 512
+NT = B // P
+NB = 2
+STACKS, PAIRS, Q = 8, 4, 16
+WIN = 448
+WSTEP = 192
+PAIR_G = ((0,), (0, 1), (0, 1), (1,))
+ZCHUNKS = (2, 2, 4, 8, 8, 8)
+GROUPS = (2, 2, 2, 2, 2, 2, 2, 1, 1)
+
+FLOPS = 2 * 2 * B * K * O
+BYTES = B * K * 2 + 3 * O * 352 * 2 + O * 2 + 2 * B * O * 4
+
+
+def unit(w, g, i):
+    if i == 0:
+        return w
+    if i == 3:
+        return 10 + w
+    return 2 + 4 * w + 2 * g + (i - 1)
+
+
+def tile_chebyshev_l3_sparsed32_stack_pa_t_kernel(tc, z, T1, T2, T0, mask, out_0, out_1):
+    nc = tc.nc
+    with ExitStack() as ctx:
+        const = ctx.enter_context(tc.tile_pool(name="const", bufs=1))
+        wpool = ctx.enter_context(tc.tile_pool(name="wpool", bufs=1))
+        zpool = ctx.enter_context(tc.tile_pool(name="zpool", bufs=1))
+        gpool = ctx.enter_context(tc.tile_pool(name="gpool", bufs=3))
+        opool = ctx.enter_context(tc.tile_pool(name="opool", bufs=5))
+        ps_t = ctx.enter_context(tc.psum_pool(name="ps_t", bufs=2))
+        ps_x = ctx.enter_context(tc.psum_pool(name="ps_x", bufs=2))
+        ps_y = ctx.enter_context(tc.psum_pool(name="ps_y", bufs=3))
+        ps_c = ctx.enter_context(tc.psum_pool(name="ps_c", bufs=1))
+        ctx.enter_context(tc.manual_schedule())
+
+        views = [a.rearrange("(s i q) k -> i q s k", s=STACKS, i=PAIRS, q=Q) for a in (mask, T1, T2)]
+        raw = []
+        for i in range(PAIRS):
+            r = wpool.tile([P, 3, WIN], BF16, name="raw%d" % i)
+            raw.append(r)
+            for a in range(3):
+                nc.sync.dma_start(out=r[:, a, :], in_=views[a][i, :, :, WSTEP * i : WSTEP * i + WIN])
+        zv = z.rearrange("(p j) k -> p j k", j=NT)
+        where = []
+        j0 = 0
+        for n, nj in enumerate(ZCHUNKS):
+            zt_sb = zpool.tile([P, nj, K], BF16, name="z%d" % n)
+            nc.sync.dma_start(out=zt_sb[:], in_=zv[:, j0 : j0 + nj, :])
+            for s in range(nj):
+                where.append((zt_sb, s))
+            j0 += nj
+
+        warm = const.tile([P, 8], F32, name="warm")
+        warm2 = const.tile([P, 8], F32, name="warm2")
+        nc.vector.memset(warm[:], 0.0)
+        nc.scalar.copy(out=warm2[:], in_=warm[:])
+        ident = const.tile([P, P], F32, name="ident")
+        make_identity(nc, ident[:])
+        t0row = const.tile([P, O], BF16, name="t0row")
+        nc.vector.memset(t0row[:].bitcast(F32), 0.0)
+        nc.scalar.dma_start(out=t0row[0:1, :], in_=T0.rearrange("(a n) -> a n", a=1))
+        ones = const.tile([P, P], BF16, name="ones")
+        nc.vector.memset(ones[:], 1.0)
+        prod = []
+        for i in range(PAIRS):
+            pr = wpool.tile([P, 2, 512 * len(PAIR_G[i])], BF16, name="prod%d" % i)
+            nc.vector.memset(pr[:].bitcast(F32), 0.0)
+            prod.append(pr)
+
+        wg = wpool.tile([P, 12, 512], BF16, name="wg", align_bytes=64)
+        wgw = wg[:].bitcast(F32)
+        wc = wpool.tile([P, 12 * P], U32, name="wc", align_bytes=64)
+        ws = wpool.tile([P, 12 * P], U8, name="ws", align_bytes=64)
+
+        def quantise_units(u0, nu):
+            nc.vector.quantize_mx(
+                out=wc[:, u0 * P : (u0 + nu) * P].bitcast(FP8X4),
+                scales=ws[:, u0 * P : (u0 + nu) * P],
+                in_=wg[:, u0 : u0 + nu, :].rearrange("p a b -> p (a b)"),
+            )
+
+        def mask_pair(i):
+            off = WSTEP * i - 512 * PAIR_G[i][0]
+            nc.vector.tensor_tensor(
+                out=prod[i][:, :, off : off + WIN],
+                in0=raw[i][:, 1:3, :],
+                in1=raw[i][:, 0:1, :].to_broadcast([P, 2, WIN]),
+                op=ALU.mult,
+            )
+
+        def flip_pair(i):
+            kbase = 512 * PAIR_G[i][0]
+            for g in PAIR_G[i]:
+                if (i + g) % 2 == 0:
+                    wt = ps_y.tile([P, 4, P], F32, name="wt", tag="y2")
+                else:
+                    wt = ps_x.tile([P, 4, P], F32, name="wt", tag="x1")
+                for w in range(2):
+                    words = prod[i][:, w, :].bitcast(F32)
+                    for u in range(2):
+                        c0 = (512 * g - kbase) // 2 + u
+                        nc.tensor.transpose(wt[:, 2 * w + u, :], words[:, c0 : c0 + 2 * P - 1 : 2], ident[:])
+                u0 = unit(0, g, i)
+                du = unit(1, g, i) - u0
+                nc.scalar.copy(
+                    out=wgw[:, u0 : u0 + du + 1 : du, :].rearrange("p w (c u) -> p w c u", u=2),
+                    in_=wt[:].rearrange("p (w u) c -> p w c u", u=2),
+                )
+
+        def quantise_pair(i):
+            if i == 0 or i == 3:
+                quantise_units(unit(0, PAIR_G[i][0], i), 2)
+            else:
+                for w in range(2):
+                    for g in range(2):
+                        quantise_units(unit(w, g, i), 1)
+
+        o0v = out_0.rearrange("(p j) o -> p j o", j=NT)
+        o1v = out_1.rearrange("(p j) o -> p j o", j=NT)
+
+        def front_flip(n):
+            zg = gpool.tile([P, NB, K], BF16, name="zg", align_bytes=64)
+            zgw = zg[:].bitcast(F32)
+            zts = []
+            for jj in range(NB):
+                src, slot = where[NB * n + jj]
+                words = src[:, slot, :].bitcast(F32)
+                zt = ps_t.tile([P, 4, P], F32, name="zt")
+                zts.append(zt)
+                for c in range(4):
+                    w0 = 2 * P * (c // 2) + c % 2
+                    nc.tensor.transpose(zt[:, c, :], words[:, w0 : w0 + 2 * P - 1 : 2], ident[:])
+            for jj in range(NB):
+                nc.scalar.copy(
+                    out=zgw[:, jj, :].rearrange("p (g b u) -> p g b u", g=2, b=P, u=2),
+                    in_=zts[jj][:].rearrange("p (g u) b -> p g b u", g=2, u=2),
+                )
+            return zg
+
+        def front_quantise(zg):
+            zc = gpool.tile([P, NB * 2 * P], U32, name="zc", align_bytes=64)
+            zs = gpool.tile([P, NB * 2 * P], U8, name="zs", align_bytes=64)
+            nc.vector.quantize_mx(
+                out=zc[:].bitcast(FP8X4), scales=zs[:], in_=zg[:].rearrange("p j k -> p (j k)")
+            )
+            return zc, zs
+
+        def passes(zc, zs):
+            accs = []
+            for jj in range(NB):
+                x1 = ps_x.tile([P, O], F32, name="x1")
+                y2 = ps_y.tile([P, O], F32, name="y2")
+                accs.append((x1, y2))
+                for w in range(2):
+                    acc = accs[jj][w]
+                    for c0, c1, g, u0, start, stop in (
+                        (0, 128, 0, unit(w, 0, 0), True, True),
+                        (128, 384, 0, unit(w, 0, 1), True, False),
+                        (128, 384, 1, unit(w, 1, 1), False, True),
+                        (384, 512, 1, unit(w, 1, 3), True, True),
+                    ):
+                        l0 = (2 * jj + g) * P
+                        r0 = u0 * P
+                        nc.tensor.matmul_mx(
+                            out=acc[:, c0:c1],
+                            lhsT=zc[:, l0 : l0 + P].bitcast(FP8X4),
+                            lhsT_scale=zs[:, l0 : l0 + P],
+                            rhs=wc[:, r0 : r0 + c1 - c0].bitcast(FP8X4),
+                            rhs_scale=ws[:, r0 : r0 + c1 - c0],
+                            start=start,
+                            stop=stop,
+                        )
+            return accs
+
+        nbunch = NT // NB
+        span = []
+        for size in GROUPS:
+            first = len(span)
+            for k in range(size):
+                span.append((first, size))
+        outs = {}
+
+        def products(n, accs):
+            first, size = span[n]
+            if n == first:
+                x1new = opool.tile([P, size * NB, O], F32, name="x1s")
+                x2new = opool.tile([P, size * NB, O], F32, name="x2s")
+                outs[first] = (x1new, x2new)
+            x1s, x2s = outs[first]
+            for jj in range(NB):
+                x1, y2 = accs[jj]
+                slot = (n - first) * NB + jj
+                nat1 = x1s[:, slot, :].rearrange("p (s r) -> p s r", s=STACKS)
+                nat2 = x2s[:, slot, :].rearrange("p (s r) -> p s r", s=STACKS)
+                nc.scalar.copy(out=nat1, in_=x1[:].rearrange("p (r s) -> p s r", s=STACKS))
+                nc.vector.scalar_tensor_tensor(
+                    out=nat2,
+                    in0=y2[:].rearrange("p (r s) -> p s r", s=STACKS),
+                    scalar=2.0,
+                    in1=nat1,
+                    op0=ALU.mult,
+                    op1=ALU.mult,
+                )
+            if n == first + size - 1:
+                nc.sync.dma_start(out=o0v[:, NB * first : NB * (first + size), :], in_=x1s[:])
+
+        def finish(n):
+            first, size = span[n]
+            x2s = outs[first][1]
+            for jj in range(NB):
+                slot = (n - first) * NB + jj
+                if jj == 1 and n < nbunch - 1:
+                    for h in range(2):
+                        cols = slice(h * (O // 2), (h + 1) * (O // 2))
+                        nc.gpsimd.tensor_tensor(
+                            out=x2s[:, slot, cols], in0=x2s[:, slot, cols], in1=t0b[:, cols], op=ALU.subtract
+                        )
+                else:
+                    nc.vector.tensor_tensor(
+                        out=x2s[:, slot, :], in0=x2s[:, slot, :], in1=t0ps[:], op=ALU.subtract
+                    )
+            if n == first + size - 1:
+                nc.sync.dma_start(out=o1v[:, NB * first : NB * (first + size), :], in_=x2s[:])
+
+        mask_pair(0)
+        flip_pair(0)
+        mask_pair(1)
+        flip_pair(1)
+        quantise_pair(0)
+        mask_pair(2)
+        flip_pair(2)
+        quantise_pair(1)
+        mask_pair(3)
+        flip_pair(3)
+        quantise_pair(2)
+        zg0 = front_flip(0)
+        quantise_pair(3)
+        cur = front_quantise(zg0)
+
+        t0ps = ps_c.tile([P, O], F32, name="t0ps")
+        nc.tensor.matmul(out=t0ps[:], lhsT=ones[:], rhs=t0row[:], start=True, stop=True)
+        t0b = const.tile([P, O], F32, name="t0b")
+        nc.scalar.copy(out=t0b[:], in_=t0ps[:])
+
+        for n in range(nbunch):
+            zg = front_flip(n + 1) if n + 1 < nbunch else None
+            accs = passes(cur[0], cur[1])
+            if zg is not None:
+                cur = front_quantise(zg)
+            if n > 0:
+                finish(n - 1)
+            products(n, accs)
+        finish(nbunch - 1)

@@ -78,7 +78,12 @@ def tile_chebyshev_l3_sparsed32_stack_pa_t_kernel(tc, z, T1, T2, T0, mask, out_0
         prod = []
         for i in range(PAIRS):
             pr = wpool.tile([P, 2, 512 * len(PAIR_G[i])], BF16, name="prod%d" % i)
-            nc.vector.memset(pr[:].bitcast(F32), 0.0)
+            prw = pr[:].bitcast(F32)
+            off = (WSTEP * i - 512 * PAIR_G[i][0]) // 2
+            if off > 0:
+                nc.vector.memset(prw[:, :, 0:off], 0.0)
+            if off + WIN // 2 < 256 * len(PAIR_G[i]):
+                nc.vector.memset(prw[:, :, off + WIN // 2 :], 0.0)
             prod.append(pr)
 
         wg = wpool.tile([P, 12, 512], BF16, name="wg", align_bytes=64)
@@ -105,7 +110,9 @@ def tile_chebyshev_l3_sparsed32_stack_pa_t_kernel(tc, z, T1, T2, T0, mask, out_0
         def flip_pair(i):
             kbase = 512 * PAIR_G[i][0]
             for g in PAIR_G[i]:
-                if (i + g) % 2 == 0:
+                if i == 3:
+                    wt = ps_c.tile([P, 4, P], F32, name="wt", tag="t0ps")
+                elif (i + g) % 2 == 0:
                     wt = ps_y.tile([P, 4, P], F32, name="wt", tag="y2")
                 else:
                     wt = ps_x.tile([P, 4, P], F32, name="wt", tag="x1")
@@ -236,19 +243,13 @@ def tile_chebyshev_l3_sparsed32_stack_pa_t_kernel(tc, z, T1, T2, T0, mask, out_0
             if n == first + size - 1:
                 nc.sync.dma_start(out=o1v[:, NB * first : NB * (first + size), :], in_=x2s[:])
 
-        mask_pair(0)
-        flip_pair(0)
-        mask_pair(1)
-        flip_pair(1)
-        quantise_pair(0)
-        mask_pair(2)
-        flip_pair(2)
-        quantise_pair(1)
-        mask_pair(3)
-        flip_pair(3)
-        quantise_pair(2)
+        for i in range(PAIRS):
+            mask_pair(i)
+        for i in range(PAIRS):
+            flip_pair(i)
+        for i in range(PAIRS):
+            quantise_pair(i)
         zg0 = front_flip(0)
-        quantise_pair(3)
         cur = front_quantise(zg0)
 
         t0ps = ps_c.tile([P, O], F32, name="t0ps")

@@ -40,6 +40,7 @@ def tile_chebyshev_l3_sparsed32_stack_pa_t_kernel(tc, z, T1, T2, T0, mask, out_0
         wpool = ctx.enter_context(tc.tile_pool(name="wpool", bufs=1))
         zpool = ctx.enter_context(tc.tile_pool(name="zpool", bufs=1))
         gpool = ctx.enter_context(tc.tile_pool(name="gpool", bufs=3))
+        ppool = ctx.enter_context(tc.tile_pool(name="ppool", bufs=3))
         opool = ctx.enter_context(tc.tile_pool(name="opool", bufs=5))
         ps_t = ctx.enter_context(tc.psum_pool(name="ps_t", bufs=2))
         ps_x = ctx.enter_context(tc.psum_pool(name="ps_x", bufs=2))
@@ -139,6 +140,17 @@ def tile_chebyshev_l3_sparsed32_stack_pa_t_kernel(tc, z, T1, T2, T0, mask, out_0
         o0v = out_0.rearrange("(p j) o -> p j o", j=NT)
         o1v = out_1.rearrange("(p j) o -> p j o", j=NT)
 
+        paired = {}
+
+        def pair_words(t):
+            src, slot = where[t]
+            zp = ppool.tile([P, 4, P], F32, name="zp")
+            nc.vector.tensor_copy(
+                out=zp[:].rearrange("p (g u) c -> p g u c", u=2),
+                in_=src[:, slot, :].bitcast(F32).rearrange("p (g c u) -> p g u c", g=2, u=2),
+            )
+            paired[t] = zp
+
         def front_flip(n):
             zg = gpool.tile([P, NB, K], BF16, name="zg", align_bytes=64)
             zgw = zg[:].bitcast(F32)
@@ -150,7 +162,11 @@ def tile_chebyshev_l3_sparsed32_stack_pa_t_kernel(tc, z, T1, T2, T0, mask, out_0
                 zts.append(zt)
                 for c in range(4):
                     w0 = 2 * P * (c // 2) + c % 2
-                    nc.tensor.transpose(zt[:, c, :], words[:, w0 : w0 + 2 * P - 1 : 2], ident[:])
+                    if NB * n + jj in paired:
+                        chunk = paired[NB * n + jj][:, c, :]
+                    else:
+                        chunk = words[:, w0 : w0 + 2 * P - 1 : 2]
+                    nc.tensor.transpose(zt[:, c, :], chunk, ident[:])
             for jj in range(NB):
                 nc.scalar.copy(
                     out=zgw[:, jj, :].rearrange("p (g b u) -> p g b u", g=2, b=P, u=2),
@@ -260,6 +276,8 @@ def tile_chebyshev_l3_sparsed32_stack_pa_t_kernel(tc, z, T1, T2, T0, mask, out_0
         for n in range(nbunch):
             zg = front_flip(n + 1) if n + 1 < nbunch else None
             accs = passes(cur[0], cur[1])
+            if n + 2 < nbunch:
+                pair_words(NB * (n + 2) + 1)
             if zg is not None:
                 cur = front_quantise(zg)
             if n > 0:

@@ -25,6 +25,9 @@ FLOPS = 2 * 2 * B * K * O
 BYTES = B * K * 2 + 3 * O * 352 * 2 + O * 2 + 2 * B * O * 4
 
 
+ON_VECTOR = ((1, 1),)
+
+
 def unit(w, g, i):
     if i == 0:
         return w
@@ -108,6 +111,8 @@ def tile_chebyshev_l3_sparsed32_stack_pa_t_kernel(tc, z, T1, T2, T0, mask, out_0
                 op=ALU.mult,
             )
 
+        late = {}
+
         def flip_pair(i):
             kbase = 512 * PAIR_G[i][0]
             for g in PAIR_G[i]:
@@ -124,10 +129,12 @@ def tile_chebyshev_l3_sparsed32_stack_pa_t_kernel(tc, z, T1, T2, T0, mask, out_0
                         nc.tensor.transpose(wt[:, 2 * w + u, :], words[:, c0 : c0 + 2 * P - 1 : 2], ident[:])
                 u0 = unit(0, g, i)
                 du = unit(1, g, i) - u0
-                nc.scalar.copy(
-                    out=wgw[:, u0 : u0 + du + 1 : du, :].rearrange("p w (c u) -> p w c u", u=2),
-                    in_=wt[:].rearrange("p (w u) c -> p w c u", u=2),
-                )
+                regrouped = wgw[:, u0 : u0 + du + 1 : du, :].rearrange("p w (c u) -> p w c u", u=2)
+                halves = wt[:].rearrange("p (w u) c -> p w c u", u=2)
+                if (i, g) in ON_VECTOR:
+                    late[(i, g)] = (regrouped, halves)
+                else:
+                    nc.scalar.copy(out=regrouped, in_=halves)
 
         def quantise_pair(i):
             if i == 0 or i == 3:
@@ -174,13 +181,18 @@ def tile_chebyshev_l3_sparsed32_stack_pa_t_kernel(tc, z, T1, T2, T0, mask, out_0
                 )
             return zg
 
-        def front_quantise(zg):
+        def codes():
             zc = gpool.tile([P, NB * 2 * P], U32, name="zc", align_bytes=64)
             zs = gpool.tile([P, NB * 2 * P], U8, name="zs", align_bytes=64)
-            nc.vector.quantize_mx(
-                out=zc[:].bitcast(FP8X4), scales=zs[:], in_=zg[:].rearrange("p j k -> p (j k)")
-            )
             return zc, zs
+
+        def quantise(zg, zc, zs, j0, j1):
+            cols = slice(2 * P * j0, 2 * P * j1)
+            nc.vector.quantize_mx(
+                out=zc[:, cols].bitcast(FP8X4),
+                scales=zs[:, cols],
+                in_=zg[:, j0:j1, :].rearrange("p j k -> p (j k)"),
+            )
 
         def passes(zc, zs):
             accs = []
@@ -246,7 +258,7 @@ def tile_chebyshev_l3_sparsed32_stack_pa_t_kernel(tc, z, T1, T2, T0, mask, out_0
             x2s = outs[first][1]
             for jj in range(NB):
                 slot = (n - first) * NB + jj
-                if jj == 1 and n < nbunch - 1:
+                if jj == 0 and n < nbunch - 1:
                     for h in range(2):
                         cols = slice(h * (O // 2), (h + 1) * (O // 2))
                         nc.gpsimd.tensor_tensor(
@@ -263,10 +275,21 @@ def tile_chebyshev_l3_sparsed32_stack_pa_t_kernel(tc, z, T1, T2, T0, mask, out_0
             mask_pair(i)
         for i in range(PAIRS):
             flip_pair(i)
-        for i in range(PAIRS):
-            quantise_pair(i)
         zg0 = front_flip(0)
-        cur = front_quantise(zg0)
+
+        def copy_late(i):
+            for g in PAIR_G[i]:
+                if (i, g) in late:
+                    nc.vector.tensor_copy(out=late[(i, g)][0], in_=late[(i, g)][1])
+
+        copy_late(1)
+        quantise_pair(0)
+        quantise_pair(1)
+        quantise_pair(2)
+        quantise_pair(3)
+        cur = codes()
+        quantise(zg0, cur[0], cur[1], 0, 1)
+        quantise(zg0, cur[0], cur[1], 1, 2)
 
         t0ps = ps_c.tile([P, O], F32, name="t0ps")
         nc.tensor.matmul(out=t0ps[:], lhsT=ones[:], rhs=t0row[:], start=True, stop=True)
@@ -278,9 +301,10 @@ def tile_chebyshev_l3_sparsed32_stack_pa_t_kernel(tc, z, T1, T2, T0, mask, out_0
             accs = passes(cur[0], cur[1])
             if n + 2 < nbunch:
                 pair_words(NB * (n + 2) + 1)
-            if zg is not None:
-                cur = front_quantise(zg)
             if n > 0:
                 finish(n - 1)
+            if zg is not None:
+                cur = codes()
+                quantise(zg, cur[0], cur[1], 0, NB)
             products(n, accs)
         finish(nbunch - 1)

@@ -43,7 +43,6 @@ def tile_chebyshev_l3_sparsed32_stack_pa_t_kernel(tc, z, T1, T2, T0, mask, out_0
         wpool = ctx.enter_context(tc.tile_pool(name="wpool", bufs=1))
         zpool = ctx.enter_context(tc.tile_pool(name="zpool", bufs=1))
         gpool = ctx.enter_context(tc.tile_pool(name="gpool", bufs=3))
-        ppool = ctx.enter_context(tc.tile_pool(name="ppool", bufs=3))
         opool = ctx.enter_context(tc.tile_pool(name="opool", bufs=5))
         ps_t = ctx.enter_context(tc.psum_pool(name="ps_t", bufs=2))
         ps_x = ctx.enter_context(tc.psum_pool(name="ps_x", bufs=2))
@@ -147,17 +146,6 @@ def tile_chebyshev_l3_sparsed32_stack_pa_t_kernel(tc, z, T1, T2, T0, mask, out_0
         o0v = out_0.rearrange("(p j) o -> p j o", j=NT)
         o1v = out_1.rearrange("(p j) o -> p j o", j=NT)
 
-        paired = {}
-
-        def pair_words(t):
-            src, slot = where[t]
-            zp = ppool.tile([P, 4, P], F32, name="zp")
-            nc.vector.tensor_copy(
-                out=zp[:].rearrange("p (g u) c -> p g u c", u=2),
-                in_=src[:, slot, :].bitcast(F32).rearrange("p (g c u) -> p g u c", g=2, u=2),
-            )
-            paired[t] = zp
-
         def front_flip(n):
             zg = gpool.tile([P, NB, K], BF16, name="zg", align_bytes=64)
             zgw = zg[:].bitcast(F32)
@@ -169,11 +157,7 @@ def tile_chebyshev_l3_sparsed32_stack_pa_t_kernel(tc, z, T1, T2, T0, mask, out_0
                 zts.append(zt)
                 for c in range(4):
                     w0 = 2 * P * (c // 2) + c % 2
-                    if NB * n + jj in paired:
-                        chunk = paired[NB * n + jj][:, c, :]
-                    else:
-                        chunk = words[:, w0 : w0 + 2 * P - 1 : 2]
-                    nc.tensor.transpose(zt[:, c, :], chunk, ident[:])
+                    nc.tensor.transpose(zt[:, c, :], words[:, w0 : w0 + 2 * P - 1 : 2], ident[:])
             for jj in range(NB):
                 nc.scalar.copy(
                     out=zgw[:, jj, :].rearrange("p (g b u) -> p g b u", g=2, b=P, u=2),
@@ -258,7 +242,7 @@ def tile_chebyshev_l3_sparsed32_stack_pa_t_kernel(tc, z, T1, T2, T0, mask, out_0
             x2s = outs[first][1]
             for jj in range(NB):
                 slot = (n - first) * NB + jj
-                if jj == 0 and n < nbunch - 1:
+                if jj == 0:
                     for h in range(2):
                         cols = slice(h * (O // 2), (h + 1) * (O // 2))
                         nc.gpsimd.tensor_tensor(
@@ -299,8 +283,6 @@ def tile_chebyshev_l3_sparsed32_stack_pa_t_kernel(tc, z, T1, T2, T0, mask, out_0
         for n in range(nbunch):
             zg = front_flip(n + 1) if n + 1 < nbunch else None
             accs = passes(cur[0], cur[1])
-            if n + 2 < nbunch:
-                pair_words(NB * (n + 2) + 1)
             if n > 0:
                 finish(n - 1)
             if zg is not None:

@@ -43,6 +43,7 @@ def tile_chebyshev_l3_sparsed32_stack_pa_t_kernel(tc, z, T1, T2, T0, mask, out_0
         wpool = ctx.enter_context(tc.tile_pool(name="wpool", bufs=1))
         zpool = ctx.enter_context(tc.tile_pool(name="zpool", bufs=1))
         gpool = ctx.enter_context(tc.tile_pool(name="gpool", bufs=3))
+        ppool = ctx.enter_context(tc.tile_pool(name="ppool", bufs=3))
         opool = ctx.enter_context(tc.tile_pool(name="opool", bufs=5))
         ps_t = ctx.enter_context(tc.psum_pool(name="ps_t", bufs=2))
         ps_x = ctx.enter_context(tc.psum_pool(name="ps_x", bufs=2))
@@ -115,9 +116,7 @@ def tile_chebyshev_l3_sparsed32_stack_pa_t_kernel(tc, z, T1, T2, T0, mask, out_0
         def flip_pair(i):
             kbase = 512 * PAIR_G[i][0]
             for g in PAIR_G[i]:
-                if i == 3:
-                    wt = ps_c.tile([P, 4, P], F32, name="wt", tag="t0ps")
-                elif (i + g) % 2 == 0:
+                if (i, g) in ((0, 0), (1, 1), (2, 1)):
                     wt = ps_y.tile([P, 4, P], F32, name="wt", tag="y2")
                 else:
                     wt = ps_x.tile([P, 4, P], F32, name="wt", tag="x1")
@@ -146,6 +145,17 @@ def tile_chebyshev_l3_sparsed32_stack_pa_t_kernel(tc, z, T1, T2, T0, mask, out_0
         o0v = out_0.rearrange("(p j) o -> p j o", j=NT)
         o1v = out_1.rearrange("(p j) o -> p j o", j=NT)
 
+        paired = {}
+
+        def pair_words(t):
+            src, slot = where[t]
+            zp = ppool.tile([P, 2, P], F32, name="zp")
+            nc.scalar.copy(
+                out=zp[:],
+                in_=src[:, slot, 0 : K // 2].bitcast(F32).rearrange("p (c u) -> p u c", u=2),
+            )
+            paired[t] = zp
+
         def front_flip(n):
             zg = gpool.tile([P, NB, K], BF16, name="zg", align_bytes=64)
             zgw = zg[:].bitcast(F32)
@@ -153,11 +163,18 @@ def tile_chebyshev_l3_sparsed32_stack_pa_t_kernel(tc, z, T1, T2, T0, mask, out_0
             for jj in range(NB):
                 src, slot = where[NB * n + jj]
                 words = src[:, slot, :].bitcast(F32)
-                zt = ps_t.tile([P, 4, P], F32, name="zt")
+                if n == 1:
+                    zt = ps_y.tile([P, 4, P], F32, name="zt", tag="y2")
+                else:
+                    zt = ps_t.tile([P, 4, P], F32, name="zt")
                 zts.append(zt)
                 for c in range(4):
                     w0 = 2 * P * (c // 2) + c % 2
-                    nc.tensor.transpose(zt[:, c, :], words[:, w0 : w0 + 2 * P - 1 : 2], ident[:])
+                    if c < 2 and NB * n + jj in paired:
+                        chunk = paired[NB * n + jj][:, c, :]
+                    else:
+                        chunk = words[:, w0 : w0 + 2 * P - 1 : 2]
+                    nc.tensor.transpose(zt[:, c, :], chunk, ident[:])
             for jj in range(NB):
                 nc.scalar.copy(
                     out=zgw[:, jj, :].rearrange("p (g b u) -> p g b u", g=2, b=P, u=2),
@@ -260,6 +277,7 @@ def tile_chebyshev_l3_sparsed32_stack_pa_t_kernel(tc, z, T1, T2, T0, mask, out_0
         for i in range(PAIRS):
             flip_pair(i)
         zg0 = front_flip(0)
+        zg1 = front_flip(1)
 
         def copy_late(i):
             for g in PAIR_G[i]:
@@ -281,7 +299,10 @@ def tile_chebyshev_l3_sparsed32_stack_pa_t_kernel(tc, z, T1, T2, T0, mask, out_0
         nc.scalar.copy(out=t0b[:], in_=t0ps[:])
 
         for n in range(nbunch):
-            zg = front_flip(n + 1) if n + 1 < nbunch else None
+            if n == 0:
+                zg = zg1
+            else:
+                zg = front_flip(n + 1) if n + 1 < nbunch else None
             accs = passes(cur[0], cur[1])
             if n > 0:
                 finish(n - 1)
@@ -289,4 +310,6 @@ def tile_chebyshev_l3_sparsed32_stack_pa_t_kernel(tc, z, T1, T2, T0, mask, out_0
                 cur = codes()
                 quantise(zg, cur[0], cur[1], 0, NB)
             products(n, accs)
+            if n + 3 < nbunch:
+                pair_words(NB * (n + 3) + 1)
         finish(nbunch - 1)

@@ -21,6 +21,8 @@ PAIR_G = ((0,), (0, 1), (0, 1), (1,))
 ZCHUNKS = (2, 2, 4, 8, 8, 8)
 GROUPS = (2, 2, 2, 2, 2, 2, 2, 1, 1)
 
+WARM = 6
+
 FLOPS = 2 * 2 * B * K * O
 BYTES = B * K * 2 + 3 * O * 352 * 2 + O * 2 + 2 * B * O * 4
 
@@ -43,7 +45,6 @@ def tile_chebyshev_l3_sparsed32_stack_pa_t_kernel(tc, z, T1, T2, T0, mask, out_0
         wpool = ctx.enter_context(tc.tile_pool(name="wpool", bufs=1))
         zpool = ctx.enter_context(tc.tile_pool(name="zpool", bufs=1))
         gpool = ctx.enter_context(tc.tile_pool(name="gpool", bufs=3))
-        ppool = ctx.enter_context(tc.tile_pool(name="ppool", bufs=3))
         opool = ctx.enter_context(tc.tile_pool(name="opool", bufs=5))
         ps_t = ctx.enter_context(tc.psum_pool(name="ps_t", bufs=2))
         ps_x = ctx.enter_context(tc.psum_pool(name="ps_x", bufs=2))
@@ -54,7 +55,7 @@ def tile_chebyshev_l3_sparsed32_stack_pa_t_kernel(tc, z, T1, T2, T0, mask, out_0
         views = [a.rearrange("(s i q) k -> i q s k", s=STACKS, i=PAIRS, q=Q) for a in (mask, T1, T2)]
         raw = []
         for i in range(PAIRS):
-            r = wpool.tile([P, 3, WIN], BF16, name="raw%d" % i)
+            r = wpool.tile([P, 3, WIN], BF16, name="raw%d" % i, align_bytes=256)
             raw.append(r)
             for a in range(3):
                 nc.sync.dma_start(out=r[:, a, :], in_=views[a][i, :, :, WSTEP * i : WSTEP * i + WIN])
@@ -62,26 +63,29 @@ def tile_chebyshev_l3_sparsed32_stack_pa_t_kernel(tc, z, T1, T2, T0, mask, out_0
         where = []
         j0 = 0
         for n, nj in enumerate(ZCHUNKS):
-            zt_sb = zpool.tile([P, nj, K], BF16, name="z%d" % n)
+            zt_sb = zpool.tile([P, nj, K], BF16, name="z%d" % n, align_bytes=256)
             nc.sync.dma_start(out=zt_sb[:], in_=zv[:, j0 : j0 + nj, :])
             for s in range(nj):
                 where.append((zt_sb, s))
             j0 += nj
 
-        warm = const.tile([P, 8], F32, name="warm")
-        warm2 = const.tile([P, 8], F32, name="warm2")
+        ones = const.tile([P, O], BF16, name="ones", align_bytes=256)
+        nc.vector.memset(ones[:], 1.0)
+        t0ps = ps_c.tile([P, O], F32, name="t0ps")
+        for k in range(WARM):
+            nc.tensor.matmul(out=t0ps[:], lhsT=ones[:, 0:P], rhs=ones[:], start=True, stop=True)
+        warm = const.tile([P, 8], F32, name="warm", align_bytes=256)
+        warm2 = const.tile([P, 8], F32, name="warm2", align_bytes=256)
         nc.vector.memset(warm[:], 0.0)
         nc.scalar.copy(out=warm2[:], in_=warm[:])
-        ident = const.tile([P, P], F32, name="ident")
+        ident = const.tile([P, P], F32, name="ident", align_bytes=256)
         make_identity(nc, ident[:])
-        t0row = const.tile([P, O], BF16, name="t0row")
+        t0row = const.tile([P, O], BF16, name="t0row", align_bytes=256)
         nc.vector.memset(t0row[:].bitcast(F32), 0.0)
         nc.scalar.dma_start(out=t0row[0:1, :], in_=T0.rearrange("(a n) -> a n", a=1))
-        ones = const.tile([P, P], BF16, name="ones")
-        nc.vector.memset(ones[:], 1.0)
         prod = []
         for i in range(PAIRS):
-            pr = wpool.tile([P, 2, 512 * len(PAIR_G[i])], BF16, name="prod%d" % i)
+            pr = wpool.tile([P, 2, 512 * len(PAIR_G[i])], BF16, name="prod%d" % i, align_bytes=256)
             prw = pr[:].bitcast(F32)
             off = (WSTEP * i - 512 * PAIR_G[i][0]) // 2
             if off > 0:
@@ -90,10 +94,10 @@ def tile_chebyshev_l3_sparsed32_stack_pa_t_kernel(tc, z, T1, T2, T0, mask, out_0
                 nc.vector.memset(prw[:, :, off + WIN // 2 :], 0.0)
             prod.append(pr)
 
-        wg = wpool.tile([P, 12, 512], BF16, name="wg", align_bytes=64)
+        wg = wpool.tile([P, 12, 512], BF16, name="wg", align_bytes=256)
         wgw = wg[:].bitcast(F32)
-        wc = wpool.tile([P, 12 * P], U32, name="wc", align_bytes=64)
-        ws = wpool.tile([P, 12 * P], U8, name="ws", align_bytes=64)
+        wc = wpool.tile([P, 12 * P], U32, name="wc", align_bytes=256)
+        ws = wpool.tile([P, 12 * P], U8, name="ws", align_bytes=256)
 
         def quantise_units(u0, nu):
             nc.vector.quantize_mx(
@@ -145,19 +149,8 @@ def tile_chebyshev_l3_sparsed32_stack_pa_t_kernel(tc, z, T1, T2, T0, mask, out_0
         o0v = out_0.rearrange("(p j) o -> p j o", j=NT)
         o1v = out_1.rearrange("(p j) o -> p j o", j=NT)
 
-        paired = {}
-
-        def pair_words(t):
-            src, slot = where[t]
-            zp = ppool.tile([P, 2, P], F32, name="zp")
-            nc.scalar.copy(
-                out=zp[:],
-                in_=src[:, slot, 0 : K // 2].bitcast(F32).rearrange("p (c u) -> p u c", u=2),
-            )
-            paired[t] = zp
-
         def front_flip(n):
-            zg = gpool.tile([P, NB, K], BF16, name="zg", align_bytes=64)
+            zg = gpool.tile([P, NB, K], BF16, name="zg", align_bytes=256)
             zgw = zg[:].bitcast(F32)
             zts = []
             for jj in range(NB):
@@ -170,11 +163,7 @@ def tile_chebyshev_l3_sparsed32_stack_pa_t_kernel(tc, z, T1, T2, T0, mask, out_0
                 zts.append(zt)
                 for c in range(4):
                     w0 = 2 * P * (c // 2) + c % 2
-                    if c < 2 and NB * n + jj in paired:
-                        chunk = paired[NB * n + jj][:, c, :]
-                    else:
-                        chunk = words[:, w0 : w0 + 2 * P - 1 : 2]
-                    nc.tensor.transpose(zt[:, c, :], chunk, ident[:])
+                    nc.tensor.transpose(zt[:, c, :], words[:, w0 : w0 + 2 * P - 1 : 2], ident[:])
             for jj in range(NB):
                 nc.scalar.copy(
                     out=zgw[:, jj, :].rearrange("p (g b u) -> p g b u", g=2, b=P, u=2),
@@ -183,8 +172,8 @@ def tile_chebyshev_l3_sparsed32_stack_pa_t_kernel(tc, z, T1, T2, T0, mask, out_0
             return zg
 
         def codes():
-            zc = gpool.tile([P, NB * 2 * P], U32, name="zc", align_bytes=64)
-            zs = gpool.tile([P, NB * 2 * P], U8, name="zs", align_bytes=64)
+            zc = gpool.tile([P, NB * 2 * P], U32, name="zc", align_bytes=256)
+            zs = gpool.tile([P, NB * 2 * P], U8, name="zs", align_bytes=256)
             return zc, zs
 
         def quantise(zg, zc, zs, j0, j1):
@@ -233,8 +222,8 @@ def tile_chebyshev_l3_sparsed32_stack_pa_t_kernel(tc, z, T1, T2, T0, mask, out_0
         def products(n, accs):
             first, size = span[n]
             if n == first:
-                x1new = opool.tile([P, size * NB, O], F32, name="x1s")
-                x2new = opool.tile([P, size * NB, O], F32, name="x2s")
+                x1new = opool.tile([P, size * NB, O], F32, name="x1s", align_bytes=256)
+                x2new = opool.tile([P, size * NB, O], F32, name="x2s", align_bytes=256)
                 outs[first] = (x1new, x2new)
             x1s, x2s = outs[first]
             for jj in range(NB):
@@ -251,7 +240,9 @@ def tile_chebyshev_l3_sparsed32_stack_pa_t_kernel(tc, z, T1, T2, T0, mask, out_0
                     op0=ALU.mult,
                     op1=ALU.mult,
                 )
-            if n == first + size - 1:
+                if n == nbunch - 1:
+                    nc.sync.dma_start(out=o0v[:, NB * n + jj, :], in_=x1s[:, slot, :])
+            if n == first + size - 1 and n < nbunch - 1:
                 nc.sync.dma_start(out=o0v[:, NB * first : NB * (first + size), :], in_=x1s[:])
 
         def finish(n):
@@ -271,6 +262,16 @@ def tile_chebyshev_l3_sparsed32_stack_pa_t_kernel(tc, z, T1, T2, T0, mask, out_0
                     )
             if n == first + size - 1:
                 nc.sync.dma_start(out=o1v[:, NB * first : NB * (first + size), :], in_=x2s[:])
+
+        def finish_last(n):
+            x2s = outs[n][1]
+            lower = slice(0, O // 2)
+            upper = slice(O // 2, O)
+            nc.gpsimd.tensor_tensor(out=x2s[:, 0, lower], in0=x2s[:, 0, lower], in1=t0b[:, lower], op=ALU.subtract)
+            nc.vector.tensor_tensor(out=x2s[:, 0, upper], in0=x2s[:, 0, upper], in1=t0ps[:, upper], op=ALU.subtract)
+            nc.sync.dma_start(out=o1v[:, NB * n, :], in_=x2s[:, 0, :])
+            nc.vector.tensor_tensor(out=x2s[:, 1, :], in0=x2s[:, 1, :], in1=t0ps[:], op=ALU.subtract)
+            nc.sync.dma_start(out=o1v[:, NB * n + 1, :], in_=x2s[:, 1, :])
 
         for i in range(PAIRS):
             mask_pair(i)
@@ -293,9 +294,8 @@ def tile_chebyshev_l3_sparsed32_stack_pa_t_kernel(tc, z, T1, T2, T0, mask, out_0
         quantise(zg0, cur[0], cur[1], 0, 1)
         quantise(zg0, cur[0], cur[1], 1, 2)
 
-        t0ps = ps_c.tile([P, O], F32, name="t0ps")
-        nc.tensor.matmul(out=t0ps[:], lhsT=ones[:], rhs=t0row[:], start=True, stop=True)
-        t0b = const.tile([P, O], F32, name="t0b")
+        nc.tensor.matmul(out=t0ps[:], lhsT=ones[:, 0:P], rhs=t0row[:], start=True, stop=True)
+        t0b = const.tile([P, O], F32, name="t0b", align_bytes=256)
         nc.scalar.copy(out=t0b[:], in_=t0ps[:])
 
         for n in range(nbunch):
@@ -310,6 +310,4 @@ def tile_chebyshev_l3_sparsed32_stack_pa_t_kernel(tc, z, T1, T2, T0, mask, out_0
                 cur = codes()
                 quantise(zg, cur[0], cur[1], 0, NB)
             products(n, accs)
-            if n + 3 < nbunch:
-                pair_words(NB * (n + 3) + 1)
-        finish(nbunch - 1)
+        finish_last(nbunch - 1)

from contextlib import ExitStack

import concourse.mybir as mybir
from concourse.masks import make_identity

F32 = mybir.dt.float32
BF16 = mybir.dt.bfloat16
U32 = mybir.dt.uint32
U8 = mybir.dt.uint8
FP8X4 = mybir.dt.float8_e4m3fn_x4
ALU = mybir.AluOpType

P = 128
B, K, O = 4096, 1024, 512
NT = B // P
NB = 2
STACKS, PAIRS, Q = 8, 4, 16
WIN = 448
WSTEP = 192
PAIR_G = ((0,), (0, 1), (0, 1), (1,))
ZCHUNKS = (2, 2, 4, 8, 8, 8)
GROUPS = (2, 2, 2, 2, 2, 2, 2, 1, 1)

WARM = 6

FLOPS = 2 * 2 * B * K * O
BYTES = B * K * 2 + 3 * O * 352 * 2 + O * 2 + 2 * B * O * 4


ON_VECTOR = ((1, 1),)


def unit(w, g, i):
    if i == 0:
        return w
    if i == 3:
        return 10 + w
    return 2 + 4 * w + 2 * g + (i - 1)


def tile_chebyshev_l3_sparsed32_stack_pa_t_kernel(tc, z, T1, T2, T0, mask, out_0, out_1):
    nc = tc.nc
    with ExitStack() as ctx:
        const = ctx.enter_context(tc.tile_pool(name="const", bufs=1))
        wpool = ctx.enter_context(tc.tile_pool(name="wpool", bufs=1))
        zpool = ctx.enter_context(tc.tile_pool(name="zpool", bufs=1))
        gpool = ctx.enter_context(tc.tile_pool(name="gpool", bufs=3))
        opool = ctx.enter_context(tc.tile_pool(name="opool", bufs=5))
        ps_t = ctx.enter_context(tc.psum_pool(name="ps_t", bufs=2))
        ps_x = ctx.enter_context(tc.psum_pool(name="ps_x", bufs=2))
        ps_y = ctx.enter_context(tc.psum_pool(name="ps_y", bufs=3))
        ps_c = ctx.enter_context(tc.psum_pool(name="ps_c", bufs=1))
        ctx.enter_context(tc.manual_schedule())

        views = [a.rearrange("(s i q) k -> i q s k", s=STACKS, i=PAIRS, q=Q) for a in (mask, T1, T2)]
        raw = []
        for i in range(PAIRS):
            r = wpool.tile([P, 3, WIN], BF16, name="raw%d" % i, align_bytes=256)
            raw.append(r)
            for a in range(3):
                nc.sync.dma_start(out=r[:, a, :], in_=views[a][i, :, :, WSTEP * i : WSTEP * i + WIN])
        zv = z.rearrange("(p j) k -> p j k", j=NT)
        where = []
        j0 = 0
        for n, nj in enumerate(ZCHUNKS):
            zt_sb = zpool.tile([P, nj, K], BF16, name="z%d" % n, align_bytes=256)
            nc.sync.dma_start(out=zt_sb[:], in_=zv[:, j0 : j0 + nj, :])
            for s in range(nj):
                where.append((zt_sb, s))
            j0 += nj

        ones = const.tile([P, O], BF16, name="ones", align_bytes=256)
        nc.vector.memset(ones[:], 1.0)
        t0ps = ps_c.tile([P, O], F32, name="t0ps")
        for k in range(WARM):
            nc.tensor.matmul(out=t0ps[:], lhsT=ones[:, 0:P], rhs=ones[:], start=True, stop=True)
        warm = const.tile([P, 8], F32, name="warm", align_bytes=256)
        warm2 = const.tile([P, 8], F32, name="warm2", align_bytes=256)
        nc.vector.memset(warm[:], 0.0)
        nc.scalar.copy(out=warm2[:], in_=warm[:])
        ident = const.tile([P, P], F32, name="ident", align_bytes=256)
        make_identity(nc, ident[:])
        t0row = const.tile([P, O], BF16, name="t0row", align_bytes=256)
        nc.vector.memset(t0row[:].bitcast(F32), 0.0)
        nc.scalar.dma_start(out=t0row[0:1, :], in_=T0.rearrange("(a n) -> a n", a=1))
        prod = []
        for i in range(PAIRS):
            pr = wpool.tile([P, 2, 512 * len(PAIR_G[i])], BF16, name="prod%d" % i, align_bytes=256)
            prw = pr[:].bitcast(F32)
            off = (WSTEP * i - 512 * PAIR_G[i][0]) // 2
            if off > 0:
                nc.vector.memset(prw[:, :, 0:off], 0.0)
            if off + WIN // 2 < 256 * len(PAIR_G[i]):
                nc.vector.memset(prw[:, :, off + WIN // 2 :], 0.0)
            prod.append(pr)

        wg = wpool.tile([P, 12, 512], BF16, name="wg", align_bytes=256)
        wgw = wg[:].bitcast(F32)
        wc = wpool.tile([P, 12 * P], U32, name="wc", align_bytes=256)
        ws = wpool.tile([P, 12 * P], U8, name="ws", align_bytes=256)

        def quantise_units(u0, nu):
            nc.vector.quantize_mx(
                out=wc[:, u0 * P : (u0 + nu) * P].bitcast(FP8X4),
                scales=ws[:, u0 * P : (u0 + nu) * P],
                in_=wg[:, u0 : u0 + nu, :].rearrange("p a b -> p (a b)"),
            )

        def mask_pair(i):
            off = WSTEP * i - 512 * PAIR_G[i][0]
            nc.vector.tensor_tensor(
                out=prod[i][:, :, off : off + WIN],
                in0=raw[i][:, 1:3, :],
                in1=raw[i][:, 0:1, :].to_broadcast([P, 2, WIN]),
                op=ALU.mult,
            )

        late = {}

        def flip_pair(i):
            kbase = 512 * PAIR_G[i][0]
            for g in PAIR_G[i]:
                if (i, g) in ((0, 0), (1, 1), (2, 1)):
                    wt = ps_y.tile([P, 4, P], F32, name="wt", tag="y2")
                else:
                    wt = ps_x.tile([P, 4, P], F32, name="wt", tag="x1")
                for w in range(2):
                    words = prod[i][:, w, :].bitcast(F32)
                    for u in range(2):
                        c0 = (512 * g - kbase) // 2 + u
                        nc.tensor.transpose(wt[:, 2 * w + u, :], words[:, c0 : c0 + 2 * P - 1 : 2], ident[:])
                u0 = unit(0, g, i)
                du = unit(1, g, i) - u0
                regrouped = wgw[:, u0 : u0 + du + 1 : du, :].rearrange("p w (c u) -> p w c u", u=2)
                halves = wt[:].rearrange("p (w u) c -> p w c u", u=2)
                if (i, g) in ON_VECTOR:
                    late[(i, g)] = (regrouped, halves)
                else:
                    nc.scalar.copy(out=regrouped, in_=halves)

        def quantise_pair(i):
            if i == 0 or i == 3:
                quantise_units(unit(0, PAIR_G[i][0], i), 2)
            else:
                for w in range(2):
                    for g in range(2):
                        quantise_units(unit(w, g, i), 1)

        o0v = out_0.rearrange("(p j) o -> p j o", j=NT)
        o1v = out_1.rearrange("(p j) o -> p j o", j=NT)

        def front_flip(n):
            zg = gpool.tile([P, NB, K], BF16, name="zg", align_bytes=256)
            zgw = zg[:].bitcast(F32)
            zts = []
            for jj in range(NB):
                src, slot = where[NB * n + jj]
                words = src[:, slot, :].bitcast(F32)
                if n == 1:
                    zt = ps_y.tile([P, 4, P], F32, name="zt", tag="y2")
                else:
                    zt = ps_t.tile([P, 4, P], F32, name="zt")
                zts.append(zt)
                for c in range(4):
                    w0 = 2 * P * (c // 2) + c % 2
                    nc.tensor.transpose(zt[:, c, :], words[:, w0 : w0 + 2 * P - 1 : 2], ident[:])
            for jj in range(NB):
                nc.scalar.copy(
                    out=zgw[:, jj, :].rearrange("p (g b u) -> p g b u", g=2, b=P, u=2),
                    in_=zts[jj][:].rearrange("p (g u) b -> p g b u", g=2, u=2),
                )
            return zg

        def codes():
            zc = gpool.tile([P, NB * 2 * P], U32, name="zc", align_bytes=256)
            zs = gpool.tile([P, NB * 2 * P], U8, name="zs", align_bytes=256)
            return zc, zs

        def quantise(zg, zc, zs, j0, j1):
            cols = slice(2 * P * j0, 2 * P * j1)
            nc.vector.quantize_mx(
                out=zc[:, cols].bitcast(FP8X4),
                scales=zs[:, cols],
                in_=zg[:, j0:j1, :].rearrange("p j k -> p (j k)"),
            )

        def passes(zc, zs):
            accs = []
            for jj in range(NB):
                x1 = ps_x.tile([P, O], F32, name="x1")
                y2 = ps_y.tile([P, O], F32, name="y2")
                accs.append((x1, y2))
                for w in range(2):
                    acc = accs[jj][w]
                    for c0, c1, g, u0, start, stop in (
                        (0, 128, 0, unit(w, 0, 0), True, True),
                        (128, 384, 0, unit(w, 0, 1), True, False),
                        (128, 384, 1, unit(w, 1, 1), False, True),
                        (384, 512, 1, unit(w, 1, 3), True, True),
                    ):
                        l0 = (2 * jj + g) * P
                        r0 = u0 * P
                        nc.tensor.matmul_mx(
                            out=acc[:, c0:c1],
                            lhsT=zc[:, l0 : l0 + P].bitcast(FP8X4),
                            lhsT_scale=zs[:, l0 : l0 + P],
                            rhs=wc[:, r0 : r0 + c1 - c0].bitcast(FP8X4),
                            rhs_scale=ws[:, r0 : r0 + c1 - c0],
                            start=start,
                            stop=stop,
                        )
            return accs

        nbunch = NT // NB
        span = []
        for size in GROUPS:
            first = len(span)
            for k in range(size):
                span.append((first, size))
        outs = {}

        def products(n, accs):
            first, size = span[n]
            if n == first:
                x1new = opool.tile([P, size * NB, O], F32, name="x1s", align_bytes=256)
                x2new = opool.tile([P, size * NB, O], F32, name="x2s", align_bytes=256)
                outs[first] = (x1new, x2new)
            x1s, x2s = outs[first]
            for jj in range(NB):
                x1, y2 = accs[jj]
                slot = (n - first) * NB + jj
                nat1 = x1s[:, slot, :].rearrange("p (s r) -> p s r", s=STACKS)
                nat2 = x2s[:, slot, :].rearrange("p (s r) -> p s r", s=STACKS)
                nc.scalar.copy(out=nat1, in_=x1[:].rearrange("p (r s) -> p s r", s=STACKS))
                nc.vector.scalar_tensor_tensor(
                    out=nat2,
                    in0=y2[:].rearrange("p (r s) -> p s r", s=STACKS),
                    scalar=2.0,
                    in1=nat1,
                    op0=ALU.mult,
                    op1=ALU.mult,
                )
                if n == nbunch - 1:
                    nc.sync.dma_start(out=o0v[:, NB * n + jj, :], in_=x1s[:, slot, :])
            if n == first + size - 1 and n < nbunch - 1:
                nc.sync.dma_start(out=o0v[:, NB * first : NB * (first + size), :], in_=x1s[:])

        def finish(n):
            first, size = span[n]
            x2s = outs[first][1]
            for jj in range(NB):
                slot = (n - first) * NB + jj
                if jj == 0:
                    for h in range(2):
                        cols = slice(h * (O // 2), (h + 1) * (O // 2))
                        nc.gpsimd.tensor_tensor(
                            out=x2s[:, slot, cols], in0=x2s[:, slot, cols], in1=t0b[:, cols], op=ALU.subtract
                        )
                else:
                    nc.vector.tensor_tensor(
                        out=x2s[:, slot, :], in0=x2s[:, slot, :], in1=t0ps[:], op=ALU.subtract
                    )
            if n == first + size - 1:
                nc.sync.dma_start(out=o1v[:, NB * first : NB * (first + size), :], in_=x2s[:])

        def finish_last(n):
            x2s = outs[n][1]
            lower = slice(0, O // 2)
            upper = slice(O // 2, O)
            nc.gpsimd.tensor_tensor(out=x2s[:, 0, lower], in0=x2s[:, 0, lower], in1=t0b[:, lower], op=ALU.subtract)
            nc.vector.tensor_tensor(out=x2s[:, 0, upper], in0=x2s[:, 0, upper], in1=t0ps[:, upper], op=ALU.subtract)
            nc.sync.dma_start(out=o1v[:, NB * n, :], in_=x2s[:, 0, :])
            nc.vector.tensor_tensor(out=x2s[:, 1, :], in0=x2s[:, 1, :], in1=t0ps[:], op=ALU.subtract)
            nc.sync.dma_start(out=o1v[:, NB * n + 1, :], in_=x2s[:, 1, :])

        for i in range(PAIRS):
            mask_pair(i)
        for i in range(PAIRS):
            flip_pair(i)
        zg0 = front_flip(0)
        zg1 = front_flip(1)

        def copy_late(i):
            for g in PAIR_G[i]:
                if (i, g) in late:
                    nc.vector.tensor_copy(out=late[(i, g)][0], in_=late[(i, g)][1])

        copy_late(1)
        quantise_pair(0)
        quantise_pair(1)
        quantise_pair(2)
        quantise_pair(3)
        cur = codes()
        quantise(zg0, cur[0], cur[1], 0, 1)
        quantise(zg0, cur[0], cur[1], 1, 2)

        nc.tensor.matmul(out=t0ps[:], lhsT=ones[:, 0:P], rhs=t0row[:], start=True, stop=True)
        t0b = const.tile([P, O], F32, name="t0b", align_bytes=256)
        nc.scalar.copy(out=t0b[:], in_=t0ps[:])

        for n in range(nbunch):
            if n == 0:
                zg = zg1
            else:
                zg = front_flip(n + 1) if n + 1 < nbunch else None
            accs = passes(cur[0], cur[1])
            if n > 0:
                finish(n - 1)
            if zg is not None:
                cur = codes()
                quantise(zg, cur[0], cur[1], 0, NB)
            products(n, accs)
        finish_last(nbunch - 1)
